import numpy as np
import ml_dtypes


def mxq(x, axis, fmt="e4m3"):
    dtype, down = {"e4m3": (ml_dtypes.float8_e4m3fn, 7), "e5m2": (ml_dtypes.float8_e5m2, 14)}[fmt]
    v = np.moveaxis(np.asarray(x, np.float32).astype(ml_dtypes.bfloat16).astype(np.float64), axis, -1)
    blocks = v.reshape(v.shape[:-1] + (-1, 32))
    amax = np.abs(blocks).max(-1, keepdims=True)
    byte = np.maximum(np.where(amax > 0, np.frexp(amax)[1] - 1 + 127, 0) - down, 1)
    scale = np.exp2(byte - 127.0)
    codes = (blocks / scale).astype(np.float32).astype(dtype).astype(np.float64)
    return np.moveaxis((codes * scale).reshape(v.shape), -1, axis)


WIDE = False


def mx_kscale(k):
    if not WIDE:
        return np.ones(k)
    levels = np.array([10, -10, 5, -5, 0])
    a = np.random.permutation(np.resize(levels, k // 512 * 4)).reshape(k // 512, 4)
    idx = np.arange(k)
    return np.exp2(a[idx // 512, idx % 128 // 32])


BF16 = ml_dtypes.bfloat16


def bf(x):
    return np.asarray(x, np.float32).astype(BF16)


def f64(x):
    return np.asarray(x).astype(np.float64)


B, I, O, M = 128, 512, 768, 2


def modemul(a, c):
    return (a.transpose(2, 3, 4, 0, 1) @ c.transpose(2, 3, 4, 0, 1)).transpose(3, 4, 0, 1, 2)


def setup_inputs():
    s = mx_kscale(I)
    sx = s[None, :, None, None, None]
    sw = s[:, None, None, None, None]
    xs, ws = (B, I, M, M, M), (I, O, M, M, M)
    return {"x_real": bf(np.random.standard_normal(xs) * sx),
            "x_imag": bf(np.random.standard_normal(xs) * sx),
            "w_real": bf(np.random.standard_normal(ws) / np.sqrt(I) / sw),
            "w_imag": bf(np.random.standard_normal(ws) / np.sqrt(I) / sw)}


def reference(x_real, x_imag, w_real, w_imag):
    xr, xi = mxq(f64(x_real), 1, "e4m3"), mxq(f64(x_imag), 1, "e4m3")
    wr, wi = mxq(f64(w_real), 0, "e4m3"), mxq(f64(w_imag), 0, "e4m3")
    re = modemul(xr, wr) - modemul(xi, wi)
    im = modemul(xr, wi) + modemul(xi, wr)
    return np.stack([re, im])

@@ -1,0 +1,174 @@
+from contextlib import ExitStack
+
+import concourse.mybir as mybir
+from concourse.masks import make_identity
+
+FLOPS = 8 * 4 * 2 * 128 * 512 * 768
+
+BF16 = mybir.dt.bfloat16
+F32 = mybir.dt.float32
+U32 = mybir.dt.uint32
+U8 = mybir.dt.uint8
+FP8X4 = mybir.dt.float8_e4m3fn_x4
+
+P = 128
+PACK = 4
+B = 128
+I = 512
+O = 768
+MODES = 8
+HALF = 4
+OC = 128
+UNITS = O // OC
+STEPS = 2 * UNITS
+
+MANUAL = True
+RG_ORDER = "p o j m"
+S_AHEAD = 2
+EV_LAG = 2
+V_TAIL = 10
+S_SHARE = ((128,128),(64,64),(64,0),(64,64),(64,0),(64,64),(64,0),(64,64),(64,0),(64,64),(64,0),(64,64))
+XE_ENGINE = "VSVSVSVS"
+
+
+def tile_mymodel_kernel(tc, x_real, x_imag, w_real, w_imag, out):
+    nc = tc.nc
+    with ExitStack() as ctx:
+        if MANUAL:
+            ctx.enter_context(tc.manual_schedule())
+        keep = ctx.enter_context(tc.tile_pool(name="keep", bufs=1))
+        big = ctx.enter_context(tc.tile_pool(name="big", bufs=2 * UNITS))
+        gpool = ctx.enter_context(tc.tile_pool(name="gpool", bufs=8))
+        qpool = ctx.enter_context(tc.tile_pool(name="qpool", bufs=8))
+        psum = ctx.enter_context(tc.psum_pool(name="psum", bufs=8))
+
+        x_raw = []
+        for name, src in (("xr", x_real), ("xi", x_imag)):
+            t = keep.tile([P, I * MODES], BF16, name="xraw_" + name)
+            nc.sync.dma_start(out=t[:], in_=src.rearrange("b i x y z -> b (i x y z)"))
+            x_raw.append(t)
+        w_raw = []
+        for u in range(UNITS):
+            pair = []
+            for name, src in (("wr", w_real), ("wi", w_imag)):
+                t = big.tile([P, PACK, OC, MODES], BF16, name="raw_%s%d" % (name, u), tag="big")
+                view = src.rearrange("(p j) o x y z -> p j o (x y z)", j=PACK)
+                nc.sync.dma_start(out=t[:], in_=view[:, :, u * OC:(u + 1) * OC, :])
+                pair.append(t)
+            w_raw.append(pair)
+
+        ident = keep.tile([P, P], F32, name="ident")
+        make_identity(nc, ident[:])
+
+        x_grp = [keep.tile([P, MODES * B * PACK], BF16, name="xg%d" % s, align_bytes=64)
+                 for s in range(3)]
+        x_codes = keep.tile([P, 3, MODES * B], U32, name="x_codes", align_bytes=64)
+        x_scales = keep.tile([P, 3, MODES * B], U8, name="x_scales", align_bytes=64)
+
+        def copy_on(engine, dst, src):
+            if engine == "S":
+                nc.scalar.copy(out=dst, in_=src)
+            else:
+                nc.vector.tensor_copy(out=dst, in_=src)
+
+        def quantise_x(s):
+            nc.vector.quantize_mx(out=x_codes[:, s, :].bitcast(FP8X4),
+                                  scales=x_scales[:, s, :], in_=x_grp[s][:])
+
+        def x_op(s, mode):
+            cols = slice(mode * B, (mode + 1) * B)
+            return x_codes[:, s, cols].bitcast(FP8X4), x_scales[:, s, cols]
+
+        x_banks = []
+        for s in range(2):
+            words = x_raw[s][:].bitcast(F32).rearrange("b (p v) -> b v p", v=16)
+            for mp in range(MODES // 2):
+                xt = psum.tile([P, PACK * B], F32, name="xt", tag="bank")
+                for t in range(PACK):
+                    nc.tensor.transpose(xt[:, t * B:(t + 1) * B], words[:, 4 * t + mp, :], ident[:])
+                x_banks.append(xt)
+        for n in range(8):
+            s, mp = n // 4, n % 4
+            src = x_banks[n][:].bitcast(BF16).rearrange("p (t b e) -> p e b t", t=PACK, b=B, e=2)
+            dst = x_grp[s][:, 2 * mp * B * PACK:(2 * mp + 2) * B * PACK].rearrange(
+                "p (e b t) -> p e b t", e=2, b=B, t=PACK)
+            copy_on(XE_ENGINE[n], dst, src)
+
+        grp = {}
+        quant = {}
+        banks = {}
+        res = {}
+        out_view = out.rearrange("c b o x y z -> b c o (x y z)")
+
+        def regroup(engine, s, v):
+            if v >= STEPS:
+                return
+            share = S_SHARE[v][s]
+            o0, o1 = (0, share) if engine == "S" else (share, OC)
+            if o0 == o1:
+                return
+            if (s, v) not in grp:
+                grp[(s, v)] = gpool.tile([P, HALF * OC * PACK], BF16, name="grp", align_bytes=64)
+            u, h = v // 2, v % 2
+            dst = grp[(s, v)][:].rearrange("p (m o j) -> " + RG_ORDER, m=HALF, o=OC, j=PACK)
+            src = w_raw[u][s][:, :, :, h * HALF:(h + 1) * HALF].rearrange("p j o m -> " + RG_ORDER)
+            copy_on(engine, dst[:, o0:o1], src[:, o0:o1])
+
+        def quantise(s, v):
+            codes = qpool.tile([P, HALF * OC], U32, name="codes", align_bytes=64)
+            scales = qpool.tile([P, HALF * OC], U8, name="scales", align_bytes=64)
+            nc.vector.quantize_mx(out=codes[:].bitcast(FP8X4), scales=scales[:], in_=grp[(s, v)][:])
+            quant[(s, v)] = (codes, scales)
+
+        def multiply(v):
+            h = v % 2
+            banks[v] = [psum.tile([P, HALF * OC], F32, name="acc%d" % c, tag="bank") for c in range(2)]
+            for m in range(HALF):
+                cols = slice(m * OC, (m + 1) * OC)
+                mode = h * HALF + m
+                for c, terms in ((0, ((0, 0), (2, 1))), (1, ((0, 1), (1, 0)))):
+                    for n, (xs, ws) in enumerate(terms):
+                        lhsT, lhsT_scale = x_op(xs, mode)
+                        codes, scales = quant[(ws, v)]
+                        nc.tensor.matmul_mx(
+                            out=banks[v][c][:, cols],
+                            lhsT=lhsT, lhsT_scale=lhsT_scale,
+                            rhs=codes[:, cols].bitcast(FP8X4), rhs_scale=scales[:, cols],
+                            start=(n == 0), stop=(n == 1))
+
+        def evacuate(v):
+            u, h = v // 2, v % 2
+            if h == 0:
+                res[u] = big.tile([P, 2, OC, MODES], F32, name="res", tag="big")
+            for c in range(2):
+                engine = "V" if (c == 0 and v >= V_TAIL) else "S"
+                copy_on(engine, res[u][:, c, :, h * HALF:(h + 1) * HALF],
+                        banks[v][c][:].rearrange("p (m o) -> p o m", m=HALF))
+            if h == 1:
+                cols = slice(u * OC, (u + 1) * OC)
+                if u < UNITS - 1:
+                    nc.sync.dma_start(out=out_view[:, :, cols, :], in_=res[u][:])
+                else:
+                    for c in range(2):
+                        nc.sync.dma_start(out=out_view[:, c, cols, :], in_=res[u][:, c, :, :])
+
+        for v in range(S_AHEAD):
+            regroup("S", 0, v)
+            regroup("S", 1, v)
+        quantise_x(0)
+        nc.vector.tensor_scalar_mul(out=x_grp[2][:], in0=x_grp[1][:], scalar1=-1.0)
+        quantise_x(1)
+        regroup("V", 0, 0)
+        quantise_x(2)
+        regroup("V", 1, 0)
+        for k in range(STEPS + EV_LAG):
+            regroup("S", 0, k + S_AHEAD)
+            regroup("S", 1, k + S_AHEAD)
+            if k < STEPS:
+                regroup("V", 0, k + 1)
+                quantise(0, k)
+                regroup("V", 1, k + 1)
+                quantise(1, k)
+                multiply(k)
+            if k >= EV_LAG:
+                evacuate(k - EV_LAG)

@@ -29,6 +29,7 @@ EV_LAG = 2
 V_TAIL = 10
 S_SHARE = ((128,128),(64,64),(64,0),(64,64),(64,0),(64,64),(64,0),(64,64),(64,0),(64,64),(64,0),(64,64))
 XE_ENGINE = "VSVSVSVS"
+LAST_SLICES = ((0, 64), (64, 96), (96, 128))
 
 
 def tile_mymodel_kernel(tc, x_real, x_imag, w_real, w_imag, out):
@@ -140,6 +141,13 @@ def tile_mymodel_kernel(tc, x_real, x_imag, w_real, w_imag, out):
             u, h = v // 2, v % 2
             if h == 0:
                 res[u] = big.tile([P, 2, OC, MODES], F32, name="res", tag="big")
+            if v == STEPS - 1:
+                for o0, o1 in LAST_SLICES:
+                    for c in range(2):
+                        copy_on("VS"[c], res[u][:, c, o0:o1, h * HALF:(h + 1) * HALF],
+                                banks[v][c][:].rearrange("p (m o) -> p o m", m=HALF)[:, o0:o1, :])
+                    nc.sync.dma_start(out=out_view[:, :, u * OC + o0:u * OC + o1, :], in_=res[u][:, :, o0:o1, :])
+                return
             for c in range(2):
                 engine = "V" if (c == 0 and v >= V_TAIL) else "S"
                 copy_on(engine, res[u][:, c, :, h * HALF:(h + 1) * HALF],

@@ -26,10 +26,11 @@ MANUAL = True
 RG_ORDER = "p o j m"
 S_AHEAD = 2
 EV_LAG = 2
-V_TAIL = 10
+V_TAIL = 11
+WARM = 6
 S_SHARE = ((128,128),(64,64),(64,0),(64,64),(64,0),(64,64),(64,0),(64,64),(64,0),(64,64),(64,0),(64,64))
 XE_ENGINE = "VSVSVSVS"
-LAST_SLICES = ((0, 64), (64, 96), (96, 128))
+LAST_SLICES = ((0, 32), (32, 64), (64, 128))
 
 
 def tile_mymodel_kernel(tc, x_real, x_imag, w_real, w_imag, out):
@@ -60,6 +61,12 @@ def tile_mymodel_kernel(tc, x_real, x_imag, w_real, w_imag, out):
 
         ident = keep.tile([P, P], F32, name="ident")
         make_identity(nc, ident[:])
+
+        zeros = keep.tile([P, 512], BF16, name="zeros")
+        nc.vector.memset(zeros[:], 0.0)
+        warm = psum.tile([P, 512], F32, name="warm", tag="bank")
+        for n in range(WARM):
+            nc.tensor.matmul(out=warm[:], lhsT=zeros[:, 0:P], rhs=zeros[:], start=True, stop=True)
 
         x_grp = [keep.tile([P, MODES * B * PACK], BF16, name="xg%d" % s, align_bytes=64)
                  for s in range(3)]
@@ -121,6 +128,17 @@ def tile_mymodel_kernel(tc, x_real, x_imag, w_real, w_imag, out):
             nc.vector.quantize_mx(out=codes[:].bitcast(FP8X4), scales=scales[:], in_=grp[(s, v)][:])
             quant[(s, v)] = (codes, scales)
 
+        def quantise_by_mode(v):
+            for s in range(2):
+                codes = qpool.tile([P, HALF * OC], U32, name="codes", align_bytes=64)
+                scales = qpool.tile([P, HALF * OC], U8, name="scales", align_bytes=64)
+                quant[(s, v)] = (codes, scales)
+            for m in range(HALF):
+                for s in range(2):
+                    codes, scales = quant[(s, v)]
+                    nc.vector.quantize_mx(out=codes[:, m * OC:(m + 1) * OC].bitcast(FP8X4), scales=scales[:, m * OC:(m + 1) * OC],
+                                          in_=grp[(s, v)][:, m * OC * PACK:(m + 1) * OC * PACK])
+
         def multiply(v):
             h = v % 2
             banks[v] = [psum.tile([P, HALF * OC], F32, name="acc%d" % c, tag="bank") for c in range(2)]
@@ -172,7 +190,16 @@ def tile_mymodel_kernel(tc, x_real, x_imag, w_real, w_imag, out):
         for k in range(STEPS + EV_LAG):
             regroup("S", 0, k + S_AHEAD)
             regroup("S", 1, k + S_AHEAD)
-            if k < STEPS:
+            if k == STEPS - 2:
+                quantise(0, k)
+                quantise(1, k)
+                multiply(k)
+                regroup("V", 0, k + 1)
+                regroup("V", 1, k + 1)
+            elif k == STEPS - 1:
+                quantise_by_mode(k)
+                multiply(k)
+            elif k < STEPS:
                 regroup("V", 0, k + 1)
                 quantise(0, k)
                 regroup("V", 1, k + 1)

@@ -28,7 +28,7 @@ S_AHEAD = 2
 EV_LAG = 2
 V_TAIL = 11
 WARM = 6
-S_SHARE = ((128,128),(64,64),(64,0),(64,64),(64,0),(64,64),(64,0),(64,64),(64,0),(64,64),(64,0),(64,64))
+S_SHARE = ((128,128),(62,62),(62,0),(62,62),(62,0),(62,62),(62,0),(62,62),(62,0),(62,62),(62,0),(62,62))
 XE_ENGINE = "VSVSVSVS"
 LAST_SLICES = ((0, 32), (32, 64), (64, 128))
 

@@ -26,7 +26,7 @@ MANUAL = True
 RG_ORDER = "p o j m"
 S_AHEAD = 2
 EV_LAG = 2
-V_TAIL = 11
+V_TAIL = 10
 WARM = 6
 S_SHARE = ((128,128),(62,62),(62,0),(62,62),(62,0),(62,62),(62,0),(62,62),(62,0),(62,62),(62,0),(62,62))
 XE_ENGINE = "VSVSVSVS"

@@ -28,7 +28,7 @@ S_AHEAD = 2
 EV_LAG = 2
 V_TAIL = 10
 WARM = 6
-S_SHARE = ((128,128),(62,62),(62,0),(62,62),(62,0),(62,62),(62,0),(62,62),(62,0),(62,62),(62,0),(62,62))
+S_SHARE = ((128,128),(60,60),(60,0),(60,60),(60,0),(60,60),(60,0),(60,60),(60,0),(60,60),(60,0),(60,60))
 XE_ENGINE = "VSVSVSVS"
 LAST_SLICES = ((0, 32), (32, 64), (64, 128))
 

@@ -22,13 +22,14 @@ OC = 128
 UNITS = O // OC
 STEPS = 2 * UNITS
 
-MANUAL = True
-RG_ORDER = "p o j m"
 S_AHEAD = 2
 EV_LAG = 2
 V_TAIL = 10
-WARM = 6
-S_SHARE = ((128,128),(60,60),(60,0),(60,60),(60,0),(60,60),(60,0),(60,60),(60,0),(60,60),(60,0),(60,60))
+WARM = 12
+PE_OC = 32
+PE_TILES = range(2, 11)
+S_SHARE = {(0, 0): 128, (1, 0): 128, (0, 1): 60, (1, 1): 60, (1, 10): 60, (1, 11): 60}
+SHARE = 52
 XE_ENGINE = "VSVSVSVS"
 LAST_SLICES = ((0, 32), (32, 64), (64, 128))
 
@@ -36,11 +37,10 @@ LAST_SLICES = ((0, 32), (32, 64), (64, 128))
 def tile_mymodel_kernel(tc, x_real, x_imag, w_real, w_imag, out):
     nc = tc.nc
     with ExitStack() as ctx:
-        if MANUAL:
-            ctx.enter_context(tc.manual_schedule())
+        ctx.enter_context(tc.manual_schedule())
         keep = ctx.enter_context(tc.tile_pool(name="keep", bufs=1))
         big = ctx.enter_context(tc.tile_pool(name="big", bufs=2 * UNITS))
-        gpool = ctx.enter_context(tc.tile_pool(name="gpool", bufs=8))
+        gpool = ctx.enter_context(tc.tile_pool(name="gpool", bufs=10))
         qpool = ctx.enter_context(tc.tile_pool(name="qpool", bufs=8))
         psum = ctx.enter_context(tc.psum_pool(name="psum", bufs=8))
 
@@ -62,11 +62,11 @@ def tile_mymodel_kernel(tc, x_real, x_imag, w_real, w_imag, out):
         ident = keep.tile([P, P], F32, name="ident")
         make_identity(nc, ident[:])
 
-        zeros = keep.tile([P, 512], BF16, name="zeros")
-        nc.vector.memset(zeros[:], 0.0)
-        warm = psum.tile([P, 512], F32, name="warm", tag="bank")
+        ident_bf = keep.tile([P, P], BF16, name="ident_bf")
+        nc.vector.tensor_copy(out=ident_bf[:], in_=ident[:])
+        warm = psum.tile([P, PACK * B], F32, name="warm", tag="bank")
         for n in range(WARM):
-            nc.tensor.matmul(out=warm[:], lhsT=zeros[:, 0:P], rhs=zeros[:], start=True, stop=True)
+            nc.tensor.transpose(warm[:, (n % PACK) * B:(n % PACK + 1) * B], ident[:], ident[:])
 
         x_grp = [keep.tile([P, MODES * B * PACK], BF16, name="xg%d" % s, align_bytes=64)
                  for s in range(3)]
@@ -103,23 +103,44 @@ def tile_mymodel_kernel(tc, x_real, x_imag, w_real, w_imag, out):
             copy_on(XE_ENGINE[n], dst, src)
 
         grp = {}
+        perm = {}
         quant = {}
         banks = {}
         res = {}
         out_view = out.rearrange("c b o x y z -> b c o (x y z)")
 
+        def grp_tile(s, v):
+            if (s, v) not in grp:
+                grp[(s, v)] = gpool.tile([P, HALF * OC * PACK], BF16, name="grp", align_bytes=64)
+            return grp[(s, v)]
+
+        def pe_regroup(s, u):
+            bank = psum.tile([P, MODES * PE_OC * PACK], BF16, name="perm", tag="bank")
+            place = bank[:].rearrange("p (m o t) -> p o t m", m=MODES, o=PE_OC, t=PACK)
+            rows = w_raw[u][s][:, :, 0:PE_OC, :].rearrange("p t o m -> p o t m")
+            for t in (0, 2):
+                nc.tensor.matmul(out=place[:, :, t:t + 2, :], lhsT=ident_bf[:], rhs=rows[:, :, t:t + 2, :],
+                                 start=True, stop=True)
+            perm[(s, u)] = bank
+
+        def pe_copy(s, u):
+            words = perm[(s, u)][:].bitcast(F32).rearrange("p (m w) -> p m w", m=MODES)
+            for h in range(2):
+                dst = grp_tile(s, 2 * u + h)[:].bitcast(F32).rearrange("p (m w) -> p m w", m=HALF)
+                nc.scalar.copy(out=dst[:, :, 0:PE_OC * PACK // 2], in_=words[:, h * HALF:(h + 1) * HALF, :])
+
         def regroup(engine, s, v):
             if v >= STEPS:
                 return
-            share = S_SHARE[v][s]
-            o0, o1 = (0, share) if engine == "S" else (share, OC)
+            share = S_SHARE.get((s, v), SHARE)
+            first = PE_OC if v // 2 * 2 + s in PE_TILES else 0
+            o0, o1 = (first, share) if engine == "S" else (share, OC)
             if o0 == o1:
                 return
-            if (s, v) not in grp:
-                grp[(s, v)] = gpool.tile([P, HALF * OC * PACK], BF16, name="grp", align_bytes=64)
+            grp_tile(s, v)
             u, h = v // 2, v % 2
-            dst = grp[(s, v)][:].rearrange("p (m o j) -> " + RG_ORDER, m=HALF, o=OC, j=PACK)
-            src = w_raw[u][s][:, :, :, h * HALF:(h + 1) * HALF].rearrange("p j o m -> " + RG_ORDER)
+            dst = grp[(s, v)][:].rearrange("p (m o j) -> " + "p o j m", m=HALF, o=OC, j=PACK)
+            src = w_raw[u][s][:, :, :, h * HALF:(h + 1) * HALF].rearrange("p j o m -> " + "p o j m")
             copy_on(engine, dst[:, o0:o1], src[:, o0:o1])
 
         def quantise(s, v):
@@ -187,9 +208,19 @@ def tile_mymodel_kernel(tc, x_real, x_imag, w_real, w_imag, out):
         regroup("V", 0, 0)
         quantise_x(2)
         regroup("V", 1, 0)
+        for s in range(2):
+            pe_regroup(s, 1)
         for k in range(STEPS + EV_LAG):
+            u = (k + S_AHEAD) // 2
+            helped = [s for s in range(2) if 2 * u + s in PE_TILES and (k + S_AHEAD) % 2 == 0]
+            if k % 2 == 1:
+                for s in range(2):
+                    if 2 * u + 2 + s in PE_TILES:
+                        pe_regroup(s, u + 1)
             regroup("S", 0, k + S_AHEAD)
             regroup("S", 1, k + S_AHEAD)
+            for s in helped:
+                pe_copy(s, u)
             if k == STEPS - 2:
                 quantise(0, k)
                 quantise(1, k)

@@ -15,23 +15,20 @@ P = 128
 PACK = 4
 B = 128
 I = 512
-O = 768
 MODES = 8
 HALF = 4
 OC = 128
-UNITS = O // OC
+UNITS = 6
 STEPS = 2 * UNITS
-
-S_AHEAD = 2
-EV_LAG = 2
-V_TAIL = 10
+AHEAD = 3
+LAG = 1
 WARM = 12
+LAST_SLICES = ((0, 32), (32, 64), (64, 128))
+FIRST_SHARE = (128, 128, 60, 60)
+SHARE = 52
 PE_OC = 32
 PE_TILES = range(2, 11)
-S_SHARE = {(0, 0): 128, (1, 0): 128, (0, 1): 60, (1, 1): 60, (1, 10): 60, (1, 11): 60}
-SHARE = 52
-XE_ENGINE = "VSVSVSVS"
-LAST_SLICES = ((0, 32), (32, 64), (64, 128))
+PE_AHEAD = 1
 
 
 def tile_mymodel_kernel(tc, x_real, x_imag, w_real, w_imag, out):
@@ -40,30 +37,31 @@ def tile_mymodel_kernel(tc, x_real, x_imag, w_real, w_imag, out):
         ctx.enter_context(tc.manual_schedule())
         keep = ctx.enter_context(tc.tile_pool(name="keep", bufs=1))
         big = ctx.enter_context(tc.tile_pool(name="big", bufs=2 * UNITS))
-        gpool = ctx.enter_context(tc.tile_pool(name="gpool", bufs=10))
-        qpool = ctx.enter_context(tc.tile_pool(name="qpool", bufs=8))
+        gpool = ctx.enter_context(tc.tile_pool(name="gpool", bufs=8))
+        qpool = ctx.enter_context(tc.tile_pool(name="qpool", bufs=12))
         psum = ctx.enter_context(tc.psum_pool(name="psum", bufs=8))
 
-        x_raw = []
-        for name, src in (("xr", x_real), ("xi", x_imag)):
-            t = keep.tile([P, I * MODES], BF16, name="xraw_" + name)
-            nc.sync.dma_start(out=t[:], in_=src.rearrange("b i x y z -> b (i x y z)"))
-            x_raw.append(t)
-        w_raw = []
+        order = [(s, v) for v in range(STEPS) for s in range(2)]
+
+        x_raw = {}
+        for s in (1, 0):
+            t = keep.tile([P, I * MODES], BF16, name="xraw_%d" % s)
+            nc.sync.dma_start(out=t[:], in_=(x_real, x_imag)[s].rearrange("b i x y z -> b (i x y z)"))
+            x_raw[s] = t
+        w_raw = {}
         for u in range(UNITS):
-            pair = []
-            for name, src in (("wr", w_real), ("wi", w_imag)):
-                t = big.tile([P, PACK, OC, MODES], BF16, name="raw_%s%d" % (name, u), tag="big")
-                view = src.rearrange("(p j) o x y z -> p j o (x y z)", j=PACK)
+            for s in range(2):
+                t = big.tile([P, PACK, OC, MODES], BF16, name="raw_%d_%d" % (s, u), tag="big")
+                view = (w_real, w_imag)[s].rearrange("(p j) o x y z -> p j o (x y z)", j=PACK)
                 nc.sync.dma_start(out=t[:], in_=view[:, :, u * OC:(u + 1) * OC, :])
-                pair.append(t)
-            w_raw.append(pair)
+                w_raw[(s, u)] = t
 
         ident = keep.tile([P, P], F32, name="ident")
         make_identity(nc, ident[:])
 
         ident_bf = keep.tile([P, P], BF16, name="ident_bf")
         nc.vector.tensor_copy(out=ident_bf[:], in_=ident[:])
+
         warm = psum.tile([P, PACK * B], F32, name="warm", tag="bank")
         for n in range(WARM):
             nc.tensor.transpose(warm[:, (n % PACK) * B:(n % PACK + 1) * B], ident[:], ident[:])
@@ -87,21 +85,6 @@ def tile_mymodel_kernel(tc, x_real, x_imag, w_real, w_imag, out):
             cols = slice(mode * B, (mode + 1) * B)
             return x_codes[:, s, cols].bitcast(FP8X4), x_scales[:, s, cols]
 
-        x_banks = []
-        for s in range(2):
-            words = x_raw[s][:].bitcast(F32).rearrange("b (p v) -> b v p", v=16)
-            for mp in range(MODES // 2):
-                xt = psum.tile([P, PACK * B], F32, name="xt", tag="bank")
-                for t in range(PACK):
-                    nc.tensor.transpose(xt[:, t * B:(t + 1) * B], words[:, 4 * t + mp, :], ident[:])
-                x_banks.append(xt)
-        for n in range(8):
-            s, mp = n // 4, n % 4
-            src = x_banks[n][:].bitcast(BF16).rearrange("p (t b e) -> p e b t", t=PACK, b=B, e=2)
-            dst = x_grp[s][:, 2 * mp * B * PACK:(2 * mp + 2) * B * PACK].rearrange(
-                "p (e b t) -> p e b t", e=2, b=B, t=PACK)
-            copy_on(XE_ENGINE[n], dst, src)
-
         grp = {}
         perm = {}
         quant = {}
@@ -109,51 +92,69 @@ def tile_mymodel_kernel(tc, x_real, x_imag, w_real, w_imag, out):
         res = {}
         out_view = out.rearrange("c b o x y z -> b c o (x y z)")
 
+        def share(i):
+            if i < len(FIRST_SHARE):
+                return FIRST_SHARE[i]
+            return SHARE
+
         def grp_tile(s, v):
             if (s, v) not in grp:
                 grp[(s, v)] = gpool.tile([P, HALF * OC * PACK], BF16, name="grp", align_bytes=64)
             return grp[(s, v)]
 
-        def pe_regroup(s, u):
+        def pe_regroup(i):
+            if i >= len(order):
+                return
+            s, v = order[i]
+            if v % 2 or v + s not in PE_TILES:
+                return
             bank = psum.tile([P, MODES * PE_OC * PACK], BF16, name="perm", tag="bank")
-            place = bank[:].rearrange("p (m o t) -> p o t m", m=MODES, o=PE_OC, t=PACK)
-            rows = w_raw[u][s][:, :, 0:PE_OC, :].rearrange("p t o m -> p o t m")
+            place = bank[:].rearrange("p (m o t) -> p t o m", m=MODES, o=PE_OC, t=PACK)
+            rows = w_raw[(s, v // 2)][:, :, 0:PE_OC, :]
             for t in (0, 2):
-                nc.tensor.matmul(out=place[:, :, t:t + 2, :], lhsT=ident_bf[:], rhs=rows[:, :, t:t + 2, :],
+                nc.tensor.matmul(out=place[:, t:t + 2, :, :], lhsT=ident_bf[:], rhs=rows[:, t:t + 2, :, :],
                                  start=True, stop=True)
-            perm[(s, u)] = bank
+            perm[(s, v)] = bank
 
-        def pe_copy(s, u):
-            words = perm[(s, u)][:].bitcast(F32).rearrange("p (m w) -> p m w", m=MODES)
+        def pe_copy(i):
+            s, v = order[i]
+            if (s, v) not in perm:
+                return
+            words = perm[(s, v)][:].bitcast(F32).rearrange("p (m w) -> p m w", m=MODES)
             for h in range(2):
-                dst = grp_tile(s, 2 * u + h)[:].bitcast(F32).rearrange("p (m w) -> p m w", m=HALF)
+                dst = grp_tile(s, v + h)[:].bitcast(F32).rearrange("p (m w) -> p m w", m=HALF)
                 nc.scalar.copy(out=dst[:, :, 0:PE_OC * PACK // 2], in_=words[:, h * HALF:(h + 1) * HALF, :])
 
-        def regroup(engine, s, v):
-            if v >= STEPS:
+        def regroup(engine, i):
+            if i >= len(order):
                 return
-            share = S_SHARE.get((s, v), SHARE)
+            s, v = order[i]
             first = PE_OC if v // 2 * 2 + s in PE_TILES else 0
-            o0, o1 = (first, share) if engine == "S" else (share, OC)
-            if o0 == o1:
-                return
-            grp_tile(s, v)
+            o0, o1 = (first, share(i)) if engine == "S" else (share(i), OC)
+            if o0 < o1:
+                regroup_span(engine, s, v, o0, o1)
+            if engine == "S":
+                pe_copy(i)
+
+        def regroup_span(engine, s, v, o0, o1):
             u, h = v // 2, v % 2
-            dst = grp[(s, v)][:].rearrange("p (m o j) -> " + "p o j m", m=HALF, o=OC, j=PACK)
-            src = w_raw[u][s][:, :, :, h * HALF:(h + 1) * HALF].rearrange("p j o m -> " + "p o j m")
+            dst = grp_tile(s, v)[:].rearrange("p (m o j) -> p o j m", m=HALF, o=OC, j=PACK)
+            src = w_raw[(s, u)][:, :, :, h * HALF:(h + 1) * HALF].rearrange("p j o m -> p o j m")
             copy_on(engine, dst[:, o0:o1], src[:, o0:o1])
 
-        def quantise(s, v):
+        def quant_tiles(s, v):
             codes = qpool.tile([P, HALF * OC], U32, name="codes", align_bytes=64)
             scales = qpool.tile([P, HALF * OC], U8, name="scales", align_bytes=64)
-            nc.vector.quantize_mx(out=codes[:].bitcast(FP8X4), scales=scales[:], in_=grp[(s, v)][:])
             quant[(s, v)] = (codes, scales)
+
+        def quantise(s, v):
+            quant_tiles(s, v)
+            codes, scales = quant[(s, v)]
+            nc.vector.quantize_mx(out=codes[:].bitcast(FP8X4), scales=scales[:], in_=grp[(s, v)][:])
 
         def quantise_by_mode(v):
             for s in range(2):
-                codes = qpool.tile([P, HALF * OC], U32, name="codes", align_bytes=64)
-                scales = qpool.tile([P, HALF * OC], U8, name="scales", align_bytes=64)
-                quant[(s, v)] = (codes, scales)
+                quant_tiles(s, v)
             for m in range(HALF):
                 for s in range(2):
                     codes, scales = quant[(s, v)]
@@ -188,53 +189,55 @@ def tile_mymodel_kernel(tc, x_real, x_imag, w_real, w_imag, out):
                     nc.sync.dma_start(out=out_view[:, :, u * OC + o0:u * OC + o1, :], in_=res[u][:, :, o0:o1, :])
                 return
             for c in range(2):
-                engine = "V" if (c == 0 and v >= V_TAIL) else "S"
+                engine = "V" if (c == 0 and v == STEPS - 2) else "S"
                 copy_on(engine, res[u][:, c, :, h * HALF:(h + 1) * HALF],
                         banks[v][c][:].rearrange("p (m o) -> p o m", m=HALF))
             if h == 1:
-                cols = slice(u * OC, (u + 1) * OC)
-                if u < UNITS - 1:
-                    nc.sync.dma_start(out=out_view[:, :, cols, :], in_=res[u][:])
-                else:
-                    for c in range(2):
-                        nc.sync.dma_start(out=out_view[:, c, cols, :], in_=res[u][:, c, :, :])
+                nc.sync.dma_start(out=out_view[:, :, u * OC:(u + 1) * OC, :], in_=res[u][:])
 
-        for v in range(S_AHEAD):
-            regroup("S", 0, v)
-            regroup("S", 1, v)
-        quantise_x(0)
-        nc.vector.tensor_scalar_mul(out=x_grp[2][:], in0=x_grp[1][:], scalar1=-1.0)
-        quantise_x(1)
-        regroup("V", 0, 0)
-        quantise_x(2)
-        regroup("V", 1, 0)
-        for s in range(2):
-            pe_regroup(s, 1)
-        for k in range(STEPS + EV_LAG):
-            u = (k + S_AHEAD) // 2
-            helped = [s for s in range(2) if 2 * u + s in PE_TILES and (k + S_AHEAD) % 2 == 0]
-            if k % 2 == 1:
-                for s in range(2):
-                    if 2 * u + 2 + s in PE_TILES:
-                        pe_regroup(s, u + 1)
-            regroup("S", 0, k + S_AHEAD)
-            regroup("S", 1, k + S_AHEAD)
-            for s in helped:
-                pe_copy(s, u)
-            if k == STEPS - 2:
-                quantise(0, k)
-                quantise(1, k)
-                multiply(k)
-                regroup("V", 0, k + 1)
-                regroup("V", 1, k + 1)
-            elif k == STEPS - 1:
-                quantise_by_mode(k)
-                multiply(k)
-            elif k < STEPS:
-                regroup("V", 0, k + 1)
-                quantise(0, k)
-                regroup("V", 1, k + 1)
-                quantise(1, k)
-                multiply(k)
-            if k >= EV_LAG:
-                evacuate(k - EV_LAG)
+        for s in (1, 0):
+            words = x_raw[s][:].bitcast(F32).rearrange("b (p v) -> b v p", v=16)
+            for mp in range(MODES // 2):
+                xt = psum.tile([P, PACK * B], F32, name="xt", tag="bank")
+                for t in range(PACK):
+                    nc.tensor.transpose(xt[:, t * B:(t + 1) * B], words[:, 4 * t + mp, :], ident[:])
+                src = xt[:].bitcast(BF16).rearrange("p (t b e) -> p e b t", t=PACK, b=B, e=2)
+                dst = x_grp[s][:, 2 * mp * B * PACK:(2 * mp + 2) * B * PACK].rearrange(
+                    "p (e b t) -> p e b t", e=2, b=B, t=PACK)
+                copy_on("VS"[mp % 2], dst, src)
+
+        for i in range(AHEAD):
+            regroup("S", i)
+        for s in (1, 0):
+            quantise_x(s)
+            if s == 1:
+                nc.vector.tensor_scalar_mul(out=x_grp[2][:], in0=x_grp[1][:], scalar1=-1.0)
+                quantise_x(2)
+        regroup("V", 0)
+
+        end = len(order) - 2
+        ready = []
+        waiting = []
+        for i, (s, v) in enumerate(order):
+            pe_regroup(i + AHEAD + PE_AHEAD)
+            regroup("S", i + AHEAD)
+            if i < end:
+                if i < end - 1:
+                    regroup("V", i + 1)
+                quantise(s, v)
+                ready.append((s, v))
+                if (1 - s, v) in ready:
+                    multiply(v)
+                    waiting.append((i, v))
+                if i == end - 1:
+                    regroup("V", end)
+            elif i == end:
+                regroup("V", end + 1)
+                quantise_by_mode(v)
+                multiply(v)
+            while waiting and waiting[0][0] <= i - LAG:
+                evacuate(waiting[0][1])
+                waiting = waiting[1:]
+        for i, v in waiting:
+            evacuate(v)
+        evacuate(STEPS - 1)

@@ -20,11 +20,12 @@ HALF = 4
 OC = 128
 UNITS = 6
 STEPS = 2 * UNITS
-AHEAD = 3
-LAG = 1
+AHEAD = 4
+LAG = 2
 WARM = 12
+X_ON_VECTOR = ((1, 0), (1, 2), (0, 0))
 LAST_SLICES = ((0, 32), (32, 64), (64, 128))
-FIRST_SHARE = (128, 128, 60, 60)
+FIRST_SHARE = (64, 64, 60, 60)
 SHARE = 52
 PE_OC = 32
 PE_TILES = range(2, 11)
@@ -204,14 +205,17 @@ def tile_mymodel_kernel(tc, x_real, x_imag, w_real, w_imag, out):
                 src = xt[:].bitcast(BF16).rearrange("p (t b e) -> p e b t", t=PACK, b=B, e=2)
                 dst = x_grp[s][:, 2 * mp * B * PACK:(2 * mp + 2) * B * PACK].rearrange(
                     "p (e b t) -> p e b t", e=2, b=B, t=PACK)
-                copy_on("VS"[mp % 2], dst, src)
+                copy_on("V" if (s, mp) in X_ON_VECTOR else "S", dst, src)
 
+        for i in range(AHEAD + PE_AHEAD):
+            pe_regroup(i)
         for i in range(AHEAD):
             regroup("S", i)
         for s in (1, 0):
-            quantise_x(s)
             if s == 1:
                 nc.vector.tensor_scalar_mul(out=x_grp[2][:], in0=x_grp[1][:], scalar1=-1.0)
+            quantise_x(s)
+            if s == 1:
                 quantise_x(2)
         regroup("V", 0)
 

@@ -28,7 +28,7 @@ LAST_SLICES = ((0, 32), (32, 64), (64, 128))
 FIRST_SHARE = (64, 64, 60, 60)
 SHARE = 52
 PE_OC = 32
-PE_TILES = range(2, 11)
+PE_BANKS = (0, 2, 2, 2, 2, 1)
 PE_AHEAD = 1
 
 
@@ -93,6 +93,9 @@ def tile_mymodel_kernel(tc, x_real, x_imag, w_real, w_imag, out):
         res = {}
         out_view = out.rearrange("c b o x y z -> b c o (x y z)")
 
+        def pe_banks(s, v):
+            return PE_BANKS[v // 2] if s == 0 else 0
+
         def share(i):
             if i < len(FIRST_SHARE):
                 return FIRST_SHARE[i]
@@ -107,31 +110,35 @@ def tile_mymodel_kernel(tc, x_real, x_imag, w_real, w_imag, out):
             if i >= len(order):
                 return
             s, v = order[i]
-            if v % 2 or v + s not in PE_TILES:
+            if v % 2:
                 return
-            bank = psum.tile([P, MODES * PE_OC * PACK], BF16, name="perm", tag="bank")
-            place = bank[:].rearrange("p (m o t) -> p t o m", m=MODES, o=PE_OC, t=PACK)
-            rows = w_raw[(s, v // 2)][:, :, 0:PE_OC, :]
-            for t in (0, 2):
-                nc.tensor.matmul(out=place[:, t:t + 2, :, :], lhsT=ident_bf[:], rhs=rows[:, t:t + 2, :, :],
-                                 start=True, stop=True)
-            perm[(s, v)] = bank
+            for n in range(pe_banks(s, v)):
+                bank = psum.tile([P, MODES * PE_OC * PACK], BF16, name="perm", tag="bank")
+                place = bank[:].rearrange("p (m o t) -> p t o m", m=MODES, o=PE_OC, t=PACK)
+                rows = w_raw[(s, v // 2)][:, :, n * PE_OC:(n + 1) * PE_OC, :]
+                for t in (0, 2):
+                    nc.tensor.matmul(out=place[:, t:t + 2, :, :], lhsT=ident_bf[:], rhs=rows[:, t:t + 2, :, :],
+                                     start=True, stop=True)
+                perm[(s, v, n)] = bank
 
         def pe_copy(i):
             s, v = order[i]
-            if (s, v) not in perm:
+            if v % 2:
                 return
-            words = perm[(s, v)][:].bitcast(F32).rearrange("p (m w) -> p m w", m=MODES)
-            for h in range(2):
-                dst = grp_tile(s, v + h)[:].bitcast(F32).rearrange("p (m w) -> p m w", m=HALF)
-                nc.scalar.copy(out=dst[:, :, 0:PE_OC * PACK // 2], in_=words[:, h * HALF:(h + 1) * HALF, :])
+            width = PE_OC * PACK // 2
+            for n in range(pe_banks(s, v)):
+                words = perm[(s, v, n)][:].bitcast(F32).rearrange("p (m w) -> p m w", m=MODES)
+                for h in range(2):
+                    dst = grp_tile(s, v + h)[:].bitcast(F32).rearrange("p (m w) -> p m w", m=HALF)
+                    nc.scalar.copy(out=dst[:, :, n * width:(n + 1) * width], in_=words[:, h * HALF:(h + 1) * HALF, :])
 
         def regroup(engine, i):
             if i >= len(order):
                 return
             s, v = order[i]
-            first = PE_OC if v // 2 * 2 + s in PE_TILES else 0
-            o0, o1 = (first, share(i)) if engine == "S" else (share(i), OC)
+            first = pe_banks(s, v) * PE_OC
+            last = max(first, share(i))
+            o0, o1 = (first, last) if engine == "S" else (last, OC)
             if o0 < o1:
                 regroup_span(engine, s, v, o0, o1)
             if engine == "S":

@@ -19,12 +19,13 @@ MODES = 8
 HALF = 4
 OC = 128
 UNITS = 6
-STEPS = 2 * UNITS
+STEPS = tuple((u, h, 0, OC) for u in range(UNITS) for h in range(2))[:-1] + ((UNITS - 1, 1, 0, OC // 2), (UNITS - 1, 1, OC // 2, OC // 2))
+LAST = len(STEPS) - 1
 AHEAD = 4
 LAG = 2
-WARM = 12
+WARM = 4
 X_ON_VECTOR = ((1, 0), (1, 2), (0, 0))
-LAST_SLICES = ((0, 32), (32, 64), (64, 128))
+LAST_SLICES = ((0, 32), (32, 64))
 FIRST_SHARE = (64, 64, 60, 60)
 SHARE = 52
 PE_OC = 32
@@ -42,7 +43,7 @@ def tile_mymodel_kernel(tc, x_real, x_imag, w_real, w_imag, out):
         qpool = ctx.enter_context(tc.tile_pool(name="qpool", bufs=12))
         psum = ctx.enter_context(tc.psum_pool(name="psum", bufs=8))
 
-        order = [(s, v) for v in range(STEPS) for s in range(2)]
+        order = [(s, v) for v in range(len(STEPS)) for s in range(2)]
 
         x_raw = {}
         for s in (1, 0):
@@ -65,7 +66,7 @@ def tile_mymodel_kernel(tc, x_real, x_imag, w_real, w_imag, out):
 
         warm = psum.tile([P, PACK * B], F32, name="warm", tag="bank")
         for n in range(WARM):
-            nc.tensor.transpose(warm[:, (n % PACK) * B:(n % PACK + 1) * B], ident[:], ident[:])
+            nc.tensor.matmul(out=warm[:, n * B:(n + 1) * B], lhsT=ident[:], rhs=ident[:], start=True, stop=True)
 
         x_grp = [keep.tile([P, MODES * B * PACK], BF16, name="xg%d" % s, align_bytes=64)
                  for s in range(3)]
@@ -94,28 +95,30 @@ def tile_mymodel_kernel(tc, x_real, x_imag, w_real, w_imag, out):
         out_view = out.rearrange("c b o x y z -> b c o (x y z)")
 
         def pe_banks(s, v):
-            return PE_BANKS[v // 2] if s == 0 else 0
+            return PE_BANKS[STEPS[v][0]] if s == 0 and STEPS[v][2] == 0 else 0
 
-        def share(i):
-            if i < len(FIRST_SHARE):
-                return FIRST_SHARE[i]
-            return SHARE
+        def span(engine, i):
+            s, v = order[i]
+            n = STEPS[v][3]
+            first = pe_banks(s, v) * PE_OC
+            last = FIRST_SHARE[i] if i < len(FIRST_SHARE) else max(first, SHARE * n // OC // 4 * 4)
+            return (first, last) if engine == "S" else (last, n)
 
         def grp_tile(s, v):
             if (s, v) not in grp:
-                grp[(s, v)] = gpool.tile([P, HALF * OC * PACK], BF16, name="grp", align_bytes=64)
+                grp[(s, v)] = gpool.tile([P, HALF * STEPS[v][3] * PACK], BF16, name="grp", align_bytes=64)
             return grp[(s, v)]
 
         def pe_regroup(i):
             if i >= len(order):
                 return
             s, v = order[i]
-            if v % 2:
+            if STEPS[v][1]:
                 return
             for n in range(pe_banks(s, v)):
                 bank = psum.tile([P, MODES * PE_OC * PACK], BF16, name="perm", tag="bank")
                 place = bank[:].rearrange("p (m o t) -> p t o m", m=MODES, o=PE_OC, t=PACK)
-                rows = w_raw[(s, v // 2)][:, :, n * PE_OC:(n + 1) * PE_OC, :]
+                rows = w_raw[(s, STEPS[v][0])][:, :, n * PE_OC:(n + 1) * PE_OC, :]
                 for t in (0, 2):
                     nc.tensor.matmul(out=place[:, t:t + 2, :, :], lhsT=ident_bf[:], rhs=rows[:, t:t + 2, :, :],
                                      start=True, stop=True)
@@ -123,7 +126,7 @@ def tile_mymodel_kernel(tc, x_real, x_imag, w_real, w_imag, out):
 
         def pe_copy(i):
             s, v = order[i]
-            if v % 2:
+            if STEPS[v][1]:
                 return
             width = PE_OC * PACK // 2
             for n in range(pe_banks(s, v)):
@@ -136,23 +139,21 @@ def tile_mymodel_kernel(tc, x_real, x_imag, w_real, w_imag, out):
             if i >= len(order):
                 return
             s, v = order[i]
-            first = pe_banks(s, v) * PE_OC
-            last = max(first, share(i))
-            o0, o1 = (first, last) if engine == "S" else (last, OC)
+            o0, o1 = span(engine, i)
             if o0 < o1:
                 regroup_span(engine, s, v, o0, o1)
             if engine == "S":
                 pe_copy(i)
 
         def regroup_span(engine, s, v, o0, o1):
-            u, h = v // 2, v % 2
-            dst = grp_tile(s, v)[:].rearrange("p (m o j) -> p o j m", m=HALF, o=OC, j=PACK)
-            src = w_raw[(s, u)][:, :, :, h * HALF:(h + 1) * HALF].rearrange("p j o m -> p o j m")
+            u, h, start, n = STEPS[v]
+            dst = grp_tile(s, v)[:].rearrange("p (m o j) -> p o j m", m=HALF, o=n, j=PACK)
+            src = w_raw[(s, u)][:, :, start:start + n, h * HALF:(h + 1) * HALF].rearrange("p j o m -> p o j m")
             copy_on(engine, dst[:, o0:o1], src[:, o0:o1])
 
         def quant_tiles(s, v):
-            codes = qpool.tile([P, HALF * OC], U32, name="codes", align_bytes=64)
-            scales = qpool.tile([P, HALF * OC], U8, name="scales", align_bytes=64)
+            codes = qpool.tile([P, HALF * STEPS[v][3]], U32, name="codes", align_bytes=64)
+            scales = qpool.tile([P, HALF * STEPS[v][3]], U8, name="scales", align_bytes=64)
             quant[(s, v)] = (codes, scales)
 
         def quantise(s, v):
@@ -160,20 +161,21 @@ def tile_mymodel_kernel(tc, x_real, x_imag, w_real, w_imag, out):
             codes, scales = quant[(s, v)]
             nc.vector.quantize_mx(out=codes[:].bitcast(FP8X4), scales=scales[:], in_=grp[(s, v)][:])
 
-        def quantise_by_mode(v):
+        def quantise_by_window(v):
             for s in range(2):
                 quant_tiles(s, v)
-            for m in range(HALF):
+            for w in range(HALF * STEPS[v][3] // OC):
                 for s in range(2):
                     codes, scales = quant[(s, v)]
-                    nc.vector.quantize_mx(out=codes[:, m * OC:(m + 1) * OC].bitcast(FP8X4), scales=scales[:, m * OC:(m + 1) * OC],
-                                          in_=grp[(s, v)][:, m * OC * PACK:(m + 1) * OC * PACK])
+                    nc.vector.quantize_mx(out=codes[:, w * OC:(w + 1) * OC].bitcast(FP8X4), scales=scales[:, w * OC:(w + 1) * OC],
+                                          in_=grp[(s, v)][:, w * OC * PACK:(w + 1) * OC * PACK])
 
         def multiply(v):
-            h = v % 2
+            u, h, start, channels = STEPS[v]
             banks[v] = [psum.tile([P, HALF * OC], F32, name="acc%d" % c, tag="bank") for c in range(2)]
             for m in range(HALF):
                 cols = slice(m * OC, (m + 1) * OC)
+                window = slice(m * channels // OC * OC, m * channels // OC * OC + OC)
                 mode = h * HALF + m
                 for c, terms in ((0, ((0, 0), (2, 1))), (1, ((0, 1), (1, 0)))):
                     for n, (xs, ws) in enumerate(terms):
@@ -182,26 +184,25 @@ def tile_mymodel_kernel(tc, x_real, x_imag, w_real, w_imag, out):
                         nc.tensor.matmul_mx(
                             out=banks[v][c][:, cols],
                             lhsT=lhsT, lhsT_scale=lhsT_scale,
-                            rhs=codes[:, cols].bitcast(FP8X4), rhs_scale=scales[:, cols],
+                            rhs=codes[:, window].bitcast(FP8X4), rhs_scale=scales[:, window],
                             start=(n == 0), stop=(n == 1))
 
         def evacuate(v):
-            u, h = v // 2, v % 2
-            if h == 0:
+            u, h, start, n = STEPS[v]
+            if h == 0 and start == 0:
                 res[u] = big.tile([P, 2, OC, MODES], F32, name="res", tag="big")
-            if v == STEPS - 1:
-                for o0, o1 in LAST_SLICES:
-                    for c in range(2):
-                        copy_on("VS"[c], res[u][:, c, o0:o1, h * HALF:(h + 1) * HALF],
-                                banks[v][c][:].rearrange("p (m o) -> p o m", m=HALF)[:, o0:o1, :])
-                    nc.sync.dma_start(out=out_view[:, :, u * OC + o0:u * OC + o1, :], in_=res[u][:, :, o0:o1, :])
-                return
-            for c in range(2):
-                engine = "V" if (c == 0 and v == STEPS - 2) else "S"
-                copy_on(engine, res[u][:, c, :, h * HALF:(h + 1) * HALF],
-                        banks[v][c][:].rearrange("p (m o) -> p o m", m=HALF))
-            if h == 1:
-                nc.sync.dma_start(out=out_view[:, :, u * OC:(u + 1) * OC, :], in_=res[u][:])
+            dst = res[u][:, :, start:start + n, h * HALF:(h + 1) * HALF]
+            for o0, o1 in LAST_SLICES if v == LAST else ((0, n),):
+                for c in range(2):
+                    engine = "V" if c == 0 and v >= LAST - 1 else "S"
+                    if n == OC:
+                        copy_on(engine, dst[:, c, o0:o1, :], banks[v][c][:].rearrange("p (m o) -> p o m", m=HALF)[:, o0:o1, :])
+                    else:
+                        src = banks[v][c][:].rearrange("p (i q o) -> p o i q", i=2, q=4, o=n)[:, o0:o1, :, 0:4:3]
+                        copy_on(engine, dst[:, c, o0:o1, :].rearrange("p o (i q) -> p o i q", i=2), src)
+                if h == 1:
+                    cols = slice(u * OC + start + o0, u * OC + start + o1)
+                    nc.sync.dma_start(out=out_view[:, :, cols, :], in_=res[u][:, :, start + o0:start + o1, :])
 
         for s in (1, 0):
             words = x_raw[s][:].bitcast(F32).rearrange("b (p v) -> b v p", v=16)
@@ -244,11 +245,11 @@ def tile_mymodel_kernel(tc, x_real, x_imag, w_real, w_imag, out):
                     regroup("V", end)
             elif i == end:
                 regroup("V", end + 1)
-                quantise_by_mode(v)
+                quantise_by_window(v)
                 multiply(v)
             while waiting and waiting[0][0] <= i - LAG:
                 evacuate(waiting[0][1])
                 waiting = waiting[1:]
         for i, v in waiting:
             evacuate(v)
-        evacuate(STEPS - 1)
+        evacuate(LAST)

@@ -25,9 +25,8 @@ AHEAD = 4
 LAG = 2
 WARM = 4
 X_ON_VECTOR = ((1, 0), (1, 2), (0, 0))
-LAST_SLICES = ((0, 32), (32, 64))
 FIRST_SHARE = (64, 64, 60, 60)
-SHARE = 52
+SHARE = 48
 PE_OC = 32
 PE_BANKS = (0, 2, 2, 2, 2, 1)
 PE_AHEAD = 1
@@ -192,17 +191,16 @@ def tile_mymodel_kernel(tc, x_real, x_imag, w_real, w_imag, out):
             if h == 0 and start == 0:
                 res[u] = big.tile([P, 2, OC, MODES], F32, name="res", tag="big")
             dst = res[u][:, :, start:start + n, h * HALF:(h + 1) * HALF]
-            for o0, o1 in LAST_SLICES if v == LAST else ((0, n),):
-                for c in range(2):
-                    engine = "V" if c == 0 and v >= LAST - 1 else "S"
-                    if n == OC:
-                        copy_on(engine, dst[:, c, o0:o1, :], banks[v][c][:].rearrange("p (m o) -> p o m", m=HALF)[:, o0:o1, :])
-                    else:
-                        src = banks[v][c][:].rearrange("p (i q o) -> p o i q", i=2, q=4, o=n)[:, o0:o1, :, 0:4:3]
-                        copy_on(engine, dst[:, c, o0:o1, :].rearrange("p o (i q) -> p o i q", i=2), src)
+            for c in range(2):
+                engine = "V" if c == 0 and v >= LAST - 1 else "S"
+                if n == OC:
+                    copy_on(engine, dst[:, c, :, :], banks[v][c][:].rearrange("p (m o) -> p o m", m=HALF))
+                else:
+                    src = banks[v][c][:].rearrange("p (i q o) -> p o i q", i=2, q=4, o=n)[:, :, :, 0:4:3]
+                    copy_on(engine, dst[:, c, :, :].rearrange("p o (i q) -> p o i q", i=2), src)
                 if h == 1:
-                    cols = slice(u * OC + start + o0, u * OC + start + o1)
-                    nc.sync.dma_start(out=out_view[:, :, cols, :], in_=res[u][:, :, start + o0:start + o1, :])
+                    cols = slice(u * OC + start, u * OC + start + n)
+                    nc.sync.dma_start(out=out_view[:, c, cols, :], in_=res[u][:, c, start:start + n, :])
 
         for s in (1, 0):
             words = x_raw[s][:].bitcast(F32).rearrange("b (p v) -> b v p", v=16)

from contextlib import ExitStack

import concourse.mybir as mybir
from concourse.masks import make_identity

FLOPS = 8 * 4 * 2 * 128 * 512 * 768

BF16 = mybir.dt.bfloat16
F32 = mybir.dt.float32
U32 = mybir.dt.uint32
U8 = mybir.dt.uint8
FP8X4 = mybir.dt.float8_e4m3fn_x4

P = 128
PACK = 4
B = 128
I = 512
MODES = 8
HALF = 4
OC = 128
UNITS = 6
STEPS = tuple((u, h, 0, OC) for u in range(UNITS) for h in range(2))[:-1] + ((UNITS - 1, 1, 0, OC // 2), (UNITS - 1, 1, OC // 2, OC // 2))
LAST = len(STEPS) - 1
AHEAD = 4
LAG = 2
WARM = 4
X_ON_VECTOR = ((1, 0), (1, 2), (0, 0))
FIRST_SHARE = (64, 64, 60, 60)
SHARE = 48
PE_OC = 32
PE_BANKS = (0, 2, 2, 2, 2, 1)
PE_AHEAD = 1


def tile_mymodel_kernel(tc, x_real, x_imag, w_real, w_imag, out):
    nc = tc.nc
    with ExitStack() as ctx:
        ctx.enter_context(tc.manual_schedule())
        keep = ctx.enter_context(tc.tile_pool(name="keep", bufs=1))
        big = ctx.enter_context(tc.tile_pool(name="big", bufs=2 * UNITS))
        gpool = ctx.enter_context(tc.tile_pool(name="gpool", bufs=8))
        qpool = ctx.enter_context(tc.tile_pool(name="qpool", bufs=12))
        psum = ctx.enter_context(tc.psum_pool(name="psum", bufs=8))

        order = [(s, v) for v in range(len(STEPS)) for s in range(2)]

        x_raw = {}
        for s in (1, 0):
            t = keep.tile([P, I * MODES], BF16, name="xraw_%d" % s)
            nc.sync.dma_start(out=t[:], in_=(x_real, x_imag)[s].rearrange("b i x y z -> b (i x y z)"))
            x_raw[s] = t
        w_raw = {}
        for u in range(UNITS):
            for s in range(2):
                t = big.tile([P, PACK, OC, MODES], BF16, name="raw_%d_%d" % (s, u), tag="big")
                view = (w_real, w_imag)[s].rearrange("(p j) o x y z -> p j o (x y z)", j=PACK)
                nc.sync.dma_start(out=t[:], in_=view[:, :, u * OC:(u + 1) * OC, :])
                w_raw[(s, u)] = t

        ident = keep.tile([P, P], F32, name="ident")
        make_identity(nc, ident[:])

        ident_bf = keep.tile([P, P], BF16, name="ident_bf")
        nc.vector.tensor_copy(out=ident_bf[:], in_=ident[:])

        warm = psum.tile([P, PACK * B], F32, name="warm", tag="bank")
        for n in range(WARM):
            nc.tensor.matmul(out=warm[:, n * B:(n + 1) * B], lhsT=ident[:], rhs=ident[:], start=True, stop=True)

        x_grp = [keep.tile([P, MODES * B * PACK], BF16, name="xg%d" % s, align_bytes=64)
                 for s in range(3)]
        x_codes = keep.tile([P, 3, MODES * B], U32, name="x_codes", align_bytes=64)
        x_scales = keep.tile([P, 3, MODES * B], U8, name="x_scales", align_bytes=64)

        def copy_on(engine, dst, src):
            if engine == "S":
                nc.scalar.copy(out=dst, in_=src)
            else:
                nc.vector.tensor_copy(out=dst, in_=src)

        def quantise_x(s):
            nc.vector.quantize_mx(out=x_codes[:, s, :].bitcast(FP8X4),
                                  scales=x_scales[:, s, :], in_=x_grp[s][:])

        def x_op(s, mode):
            cols = slice(mode * B, (mode + 1) * B)
            return x_codes[:, s, cols].bitcast(FP8X4), x_scales[:, s, cols]

        grp = {}
        perm = {}
        quant = {}
        banks = {}
        res = {}
        out_view = out.rearrange("c b o x y z -> b c o (x y z)")

        def pe_banks(s, v):
            return PE_BANKS[STEPS[v][0]] if s == 0 and STEPS[v][2] == 0 else 0

        def span(engine, i):
            s, v = order[i]
            n = STEPS[v][3]
            first = pe_banks(s, v) * PE_OC
            last = FIRST_SHARE[i] if i < len(FIRST_SHARE) else max(first, SHARE * n // OC // 4 * 4)
            return (first, last) if engine == "S" else (last, n)

        def grp_tile(s, v):
            if (s, v) not in grp:
                grp[(s, v)] = gpool.tile([P, HALF * STEPS[v][3] * PACK], BF16, name="grp", align_bytes=64)
            return grp[(s, v)]

        def pe_regroup(i):
            if i >= len(order):
                return
            s, v = order[i]
            if STEPS[v][1]:
                return
            for n in range(pe_banks(s, v)):
                bank = psum.tile([P, MODES * PE_OC * PACK], BF16, name="perm", tag="bank")
                place = bank[:].rearrange("p (m o t) -> p t o m", m=MODES, o=PE_OC, t=PACK)
                rows = w_raw[(s, STEPS[v][0])][:, :, n * PE_OC:(n + 1) * PE_OC, :]
                for t in (0, 2):
                    nc.tensor.matmul(out=place[:, t:t + 2, :, :], lhsT=ident_bf[:], rhs=rows[:, t:t + 2, :, :],
                                     start=True, stop=True)
                perm[(s, v, n)] = bank

        def pe_copy(i):
            s, v = order[i]
            if STEPS[v][1]:
                return
            width = PE_OC * PACK // 2
            for n in range(pe_banks(s, v)):
                words = perm[(s, v, n)][:].bitcast(F32).rearrange("p (m w) -> p m w", m=MODES)
                for h in range(2):
                    dst = grp_tile(s, v + h)[:].bitcast(F32).rearrange("p (m w) -> p m w", m=HALF)
                    nc.scalar.copy(out=dst[:, :, n * width:(n + 1) * width], in_=words[:, h * HALF:(h + 1) * HALF, :])

        def regroup(engine, i):
            if i >= len(order):
                return
            s, v = order[i]
            o0, o1 = span(engine, i)
            if o0 < o1:
                regroup_span(engine, s, v, o0, o1)
            if engine == "S":
                pe_copy(i)

        def regroup_span(engine, s, v, o0, o1):
            u, h, start, n = STEPS[v]
            dst = grp_tile(s, v)[:].rearrange("p (m o j) -> p o j m", m=HALF, o=n, j=PACK)
            src = w_raw[(s, u)][:, :, start:start + n, h * HALF:(h + 1) * HALF].rearrange("p j o m -> p o j m")
            copy_on(engine, dst[:, o0:o1], src[:, o0:o1])

        def quant_tiles(s, v):
            codes = qpool.tile([P, HALF * STEPS[v][3]], U32, name="codes", align_bytes=64)
            scales = qpool.tile([P, HALF * STEPS[v][3]], U8, name="scales", align_bytes=64)
            quant[(s, v)] = (codes, scales)

        def quantise(s, v):
            quant_tiles(s, v)
            codes, scales = quant[(s, v)]
            nc.vector.quantize_mx(out=codes[:].bitcast(FP8X4), scales=scales[:], in_=grp[(s, v)][:])

        def quantise_by_window(v):
            for s in range(2):
                quant_tiles(s, v)
            for w in range(HALF * STEPS[v][3] // OC):
                for s in range(2):
                    codes, scales = quant[(s, v)]
                    nc.vector.quantize_mx(out=codes[:, w * OC:(w + 1) * OC].bitcast(FP8X4), scales=scales[:, w * OC:(w + 1) * OC],
                                          in_=grp[(s, v)][:, w * OC * PACK:(w + 1) * OC * PACK])

        def multiply(v):
            u, h, start, channels = STEPS[v]
            banks[v] = [psum.tile([P, HALF * OC], F32, name="acc%d" % c, tag="bank") for c in range(2)]
            for m in range(HALF):
                cols = slice(m * OC, (m + 1) * OC)
                window = slice(m * channels // OC * OC, m * channels // OC * OC + OC)
                mode = h * HALF + m
                for c, terms in ((0, ((0, 0), (2, 1))), (1, ((0, 1), (1, 0)))):
                    for n, (xs, ws) in enumerate(terms):
                        lhsT, lhsT_scale = x_op(xs, mode)
                        codes, scales = quant[(ws, v)]
                        nc.tensor.matmul_mx(
                            out=banks[v][c][:, cols],
                            lhsT=lhsT, lhsT_scale=lhsT_scale,
                            rhs=codes[:, window].bitcast(FP8X4), rhs_scale=scales[:, window],
                            start=(n == 0), stop=(n == 1))

        def evacuate(v):
            u, h, start, n = STEPS[v]
            if h == 0 and start == 0:
                res[u] = big.tile([P, 2, OC, MODES], F32, name="res", tag="big")
            dst = res[u][:, :, start:start + n, h * HALF:(h + 1) * HALF]
            for c in range(2):
                engine = "V" if c == 0 and v >= LAST - 1 else "S"
                if n == OC:
                    copy_on(engine, dst[:, c, :, :], banks[v][c][:].rearrange("p (m o) -> p o m", m=HALF))
                else:
                    src = banks[v][c][:].rearrange("p (i q o) -> p o i q", i=2, q=4, o=n)[:, :, :, 0:4:3]
                    copy_on(engine, dst[:, c, :, :].rearrange("p o (i q) -> p o i q", i=2), src)
                if h == 1:
                    cols = slice(u * OC + start, u * OC + start + n)
                    nc.sync.dma_start(out=out_view[:, c, cols, :], in_=res[u][:, c, start:start + n, :])

        for s in (1, 0):
            words = x_raw[s][:].bitcast(F32).rearrange("b (p v) -> b v p", v=16)
            for mp in range(MODES // 2):
                xt = psum.tile([P, PACK * B], F32, name="xt", tag="bank")
                for t in range(PACK):
                    nc.tensor.transpose(xt[:, t * B:(t + 1) * B], words[:, 4 * t + mp, :], ident[:])
                src = xt[:].bitcast(BF16).rearrange("p (t b e) -> p e b t", t=PACK, b=B, e=2)
                dst = x_grp[s][:, 2 * mp * B * PACK:(2 * mp + 2) * B * PACK].rearrange(
                    "p (e b t) -> p e b t", e=2, b=B, t=PACK)
                copy_on("V" if (s, mp) in X_ON_VECTOR else "S", dst, src)

        for i in range(AHEAD + PE_AHEAD):
            pe_regroup(i)
        for i in range(AHEAD):
            regroup("S", i)
        for s in (1, 0):
            if s == 1:
                nc.vector.tensor_scalar_mul(out=x_grp[2][:], in0=x_grp[1][:], scalar1=-1.0)
            quantise_x(s)
            if s == 1:
                quantise_x(2)
        regroup("V", 0)

        end = len(order) - 2
        ready = []
        waiting = []
        for i, (s, v) in enumerate(order):
            pe_regroup(i + AHEAD + PE_AHEAD)
            regroup("S", i + AHEAD)
            if i < end:
                if i < end - 1:
                    regroup("V", i + 1)
                quantise(s, v)
                ready.append((s, v))
                if (1 - s, v) in ready:
                    multiply(v)
                    waiting.append((i, v))
                if i == end - 1:
                    regroup("V", end)
            elif i == end:
                regroup("V", end + 1)
                quantise_by_window(v)
                multiply(v)
            while waiting and waiting[0][0] <= i - LAG:
                evacuate(waiting[0][1])
                waiting = waiting[1:]
        for i, v in waiting:
            evacuate(v)
        evacuate(LAST)
